import numpy as np
import ml_dtypes


def mxq(x, axis, fmt="e4m3"):
    dtype, down = {"e4m3": (ml_dtypes.float8_e4m3fn, 7), "e5m2": (ml_dtypes.float8_e5m2, 14)}[fmt]
    v = np.moveaxis(np.asarray(x, np.float32).astype(ml_dtypes.bfloat16).astype(np.float64), axis, -1)
    blocks = v.reshape(v.shape[:-1] + (-1, 32))
    amax = np.abs(blocks).max(-1, keepdims=True)
    byte = np.maximum(np.where(amax > 0, np.frexp(amax)[1] - 1 + 127, 0) - down, 1)
    scale = np.exp2(byte - 127.0)
    codes = (blocks / scale).astype(np.float32).astype(dtype).astype(np.float64)
    return np.moveaxis((codes * scale).reshape(v.shape), -1, axis)


WIDE = False


def mx_kscale(k):
    if not WIDE:
        return np.ones(k)
    levels = np.array([10, -10, 5, -5, 0])
    a = np.random.permutation(np.resize(levels, k // 512 * 4)).reshape(k // 512, 4)
    idx = np.arange(k)
    return np.exp2(a[idx // 512, idx % 128 // 32])


BF16 = ml_dtypes.bfloat16


def bf(x):
    return np.asarray(x, np.float32).astype(BF16)


def f64(x):
    return np.asarray(x).astype(np.float64)


BS, N, D, B, D_PM = 2, 1024, 1024, 8, 512
BUDGET = 16.0


def sigmoid(v):
    return 1.0 / (1.0 + np.exp(-v))


def softplus(v):
    return np.log(1.0 + np.exp(v))


def setup_inputs():
    k = mx_kscale(D_PM)
    a = np.random.standard_normal((BS, N, D_PM))
    g = 0.5 * a.transpose(0, 2, 1) @ a / N
    f = np.exp(0.4 * np.random.standard_normal((BS, B, 1, 1)))
    w = np.eye(D_PM) / B + 0.8 * BUDGET / D_PM * f * np.random.standard_normal((BS, B, D_PM, D_PM))
    return {"W_pm": bf(w * k),
            "G": bf(g * k / k[:, None]),
            "raw_beta": bf(0.5 * np.random.standard_normal(B)),
            "raw_decay": bf(1.5 + 0.5 * np.random.standard_normal(B))}


def reference(W_pm, G, raw_beta, raw_decay):
    beta = softplus(f64(raw_beta))
    decay = sigmoid(f64(raw_decay))
    T = decay[None, :, None, None] * np.eye(D_PM) + beta[None, :, None, None] * f64(G)[:, None]
    W_new = mxq(f64(W_pm), 3, "e4m3") @ mxq(T, 2, "e4m3")
    frob = np.sqrt(np.sum(W_new * W_new, axis=(-2, -1), keepdims=True))
    scale = np.minimum(BUDGET / np.maximum(frob, 1e-8), 1.0)
    return W_new * scale

@@ -1,0 +1,274 @@
+from contextlib import ExitStack
+
+import concourse.bass as bass
+import concourse.mybir as mybir
+import concourse.tile as tile
+from concourse.masks import make_identity
+
+F32 = mybir.dt.float32
+BF16 = mybir.dt.bfloat16
+U32 = mybir.dt.uint32
+U8 = mybir.dt.uint8
+FP8X4 = mybir.dt.float8_e4m3fn_x4
+ACT = mybir.ActivationFunctionType
+ALU = mybir.AluOpType
+
+P = 128
+D = 512
+NB = 8
+NM = 16
+FREE = 4 * D
+BUDGET = 16.0
+
+FLOPS = 2 * NM * D * D * D
+
+W_BUFS = 8
+W_AHEAD = 6
+
+
+def tile_proceduralmemory_pb_kernel(tc, W_pm, G, raw_beta, raw_decay, out):
+    nc = tc.nc
+    with ExitStack() as ctx:
+        const = ctx.enter_context(tc.tile_pool(name="const", bufs=1))
+        wpool = ctx.enter_context(tc.tile_pool(name="wpool", bufs=W_BUFS))
+        stage = ctx.enter_context(tc.tile_pool(name="stage", bufs=3))
+        codes = ctx.enter_context(tc.tile_pool(name="codes", bufs=4))
+        small = ctx.enter_context(tc.tile_pool(name="small", bufs=4))
+        opool = ctx.enter_context(tc.tile_pool(name="opool", bufs=4))
+        junkp = ctx.enter_context(tc.tile_pool(name="junkp", bufs=2))
+        ptp = ctx.enter_context(tc.psum_pool(name="ptp", bufs=2))
+        pu = ctx.enter_context(tc.psum_pool(name="pu", bufs=5))
+        ptot = ctx.enter_context(tc.psum_pool(name="ptot", bufs=1))
+
+        rb = const.tile([P, NB], BF16, name="rb")
+        rd = const.tile([P, NB], BF16, name="rd")
+        nc.scalar.dma_start(out=rb[:], in_=raw_beta.partition_broadcast(P))
+        nc.scalar.dma_start(out=rd[:], in_=raw_decay.partition_broadcast(P))
+
+        g_n = []
+        g_r = []
+        for b in range(2):
+            g_n.append(const.tile([P, FREE], BF16, name="g_n%d" % b))
+            g_r.append(const.tile([P, FREE], BF16, name="g_r%d" % b))
+
+        def load_g(b):
+            nc.sync.dma_start(
+                out=g_n[b][:].rearrange("p (u x) -> p u x", u=2),
+                in_=G[b].rearrange("(u q e) n -> q u (e n)", u=2, e=2),
+            )
+
+        w_sb = {}
+
+        def load_w(m):
+            b, k = divmod(m, NB)
+            t = wpool.tile([P, FREE], BF16, name="w_sb", tag="w_sb")
+            nc.sync.dma_start(out=t[:], in_=W_pm[b, k].rearrange("(p a) j -> p (a j)", a=4))
+            w_sb[m] = t
+
+        load_g(0)
+        load_w(0)
+        load_w(1)
+        load_w(2)
+        load_g(1)
+        for m in range(3, W_AHEAD):
+            load_w(m)
+
+        ident = const.tile([P, P], F32, name="ident")
+        make_identity(nc, ident[:])
+        ones = const.tile([P, P], F32, name="ones")
+        nc.vector.memset(ones[:], 1.0)
+        one_col = const.tile([P, 1], F32, name="one_col")
+        nc.vector.memset(one_col[:], 1.0)
+        neg_col = const.tile([P, 1], F32, name="neg_col")
+        nc.vector.memset(neg_col[:], -1.0)
+
+        eye_r = const.tile([P, FREE], BF16, name="eye_r")
+        nc.vector.memset(eye_r[:], 0.0)
+        eye_v = eye_r[:].rearrange("p (c n x) -> p c n x", c=2, n=P, x=8)
+        for u in range(2):
+            for e in range(2):
+                nc.vector.tensor_copy(out=eye_v[:, u, :, 5 * e + 2 * u], in_=ident[:])
+
+        warm = const.tile([P, 1], F32, name="warm")
+        nc.scalar.activation(out=warm[:], in_=one_col[:], func=ACT.Exp)
+        ab = const.tile([P, NB], F32, name="ab")
+        nc.scalar.activation(out=ab[:], in_=rb[:], func=ACT.Abs)
+        e2 = const.tile([P, NB], F32, name="e2")
+        nc.scalar.activation(out=e2[:], in_=rd[:], func=ACT.Exp, scale=-1.0)
+        e1 = const.tile([P, NB], F32, name="e1")
+        nc.scalar.activation(out=e1[:], in_=ab[:], func=ACT.Exp, scale=-1.0)
+        l1 = const.tile([P, NB], F32, name="l1")
+        nc.scalar.activation(out=l1[:], in_=e1[:], func=ACT.Ln, bias=one_col[:])
+        warm2 = const.tile([P, 1], F32, name="warm2")
+        nc.scalar.activation(out=warm2[:], in_=l1[:, 0:1], func=ACT.Sqrt, bias=one_col[:])
+
+        d1 = const.tile([P, NB], F32, name="d1")
+        nc.vector.tensor_scalar_add(out=d1[:], in0=e2[:], scalar1=1.0)
+        decay = const.tile([P, NB], F32, name="decay")
+        nc.vector.reciprocal(out=decay[:], in_=d1[:])
+        beta = const.tile([P, NB], F32, name="beta")
+        nc.vector.scalar_tensor_tensor(
+            out=beta[:], in0=rb[:], scalar=0.0, in1=l1[:], op0=ALU.max, op1=ALU.add
+        )
+
+        dk = []
+        for k in range(NB):
+            dk.append(const.tile([P, FREE], F32, name="dk%d" % k))
+
+        tot = ptot.tile([P, NM], F32, name="tot")
+
+        def regroup_g(b):
+            nc.vector.tensor_copy(
+                out=g_r[b][:].rearrange("p (n t) -> p n t", t=4),
+                in_=g_n[b][:].rearrange("p (t n) -> p n t", t=4),
+            )
+
+        tps = {}
+        wg = {}
+        tbf = {}
+        wcod = {}
+        wscl = {}
+        tcod = {}
+        tscl = {}
+        acc = {}
+        sfac = {}
+        yrel = {}
+        fsq = {}
+        o_sb = {}
+
+        def transposes(m):
+            x32 = w_sb[m][:].bitcast(F32)
+            tiles = []
+            for h in range(2):
+                tp = ptp.tile([P, 2, 2, P], F32, name="tp", tag="tp")
+                for al in range(2):
+                    a = 2 * h + al
+                    for u in range(2):
+                        c0 = a * 256 + u * P
+                        nc.tensor.transpose(tp[:, al, u, :], x32[:, c0 : c0 + P], ident[:])
+                tiles.append(tp)
+            tps[m] = tiles
+
+        def evac(m):
+            g = stage.tile([P, FREE], BF16, name="wg", tag="wg", align_bytes=64)
+            g32 = g[:].bitcast(F32).rearrange("p (a m u) -> p a m u", a=4, m=P, u=2)
+            for h in range(2):
+                nc.vector.tensor_copy(
+                    out=g32[:, 2 * h : 2 * h + 2],
+                    in_=tps[m][h][:].rearrange("p a u m -> p a m u"),
+                )
+            wg[m] = g
+
+        def quant_w(m):
+            c = codes.tile([P, D], U32, name="wcod", tag="wcod", align_bytes=64)
+            s = codes.tile([P, D], U8, name="wscl", tag="wscl", align_bytes=64)
+            nc.vector.quantize_mx(out=c[:].bitcast(FP8X4), scales=s[:], in_=wg[m][:])
+            wcod[m] = c
+            wscl[m] = s
+
+        def tcomp(m):
+            b, k = divmod(m, NB)
+            if b == 0:
+                nc.vector.tensor_scalar(
+                    out=dk[k][:], in0=eye_r[:], scalar1=decay[:, k : k + 1], scalar2=None, op0=ALU.mult
+                )
+            t = stage.tile([P, FREE], BF16, name="tbf", tag="tbf", align_bytes=64)
+            nc.vector.scalar_tensor_tensor(
+                out=t[:], in0=g_r[b][:], scalar=beta[:, k : k + 1], in1=dk[k][:],
+                op0=ALU.mult, op1=ALU.add,
+            )
+            tbf[m] = t
+
+        def quant_t(m):
+            c = codes.tile([P, D], U32, name="tcod", tag="tcod", align_bytes=64)
+            s = codes.tile([P, D], U8, name="tscl", tag="tscl", align_bytes=64)
+            nc.vector.quantize_mx(out=c[:].bitcast(FP8X4), scales=s[:], in_=tbf[m][:])
+            tcod[m] = c
+            tscl[m] = s
+
+        def prep_step(j):
+            if j < NM:
+                if j % NB == 0:
+                    regroup_g(j // NB)
+                transposes(j)
+                if j + W_AHEAD < NM:
+                    load_w(j + W_AHEAD)
+                evac(j)
+            if 1 <= j <= NM:
+                quant_t(j - 1)
+            if j < NM:
+                tcomp(j)
+                quant_w(j)
+
+        def mx_pass(m, a):
+            u = pu.tile([P, D], F32, name="u", tag="u")
+            nc.tensor.matmul_mx(
+                out=u[:],
+                lhsT=wcod[m][:, a * P : (a + 1) * P].bitcast(FP8X4),
+                lhsT_scale=wscl[m][:, a * P : (a + 1) * P],
+                rhs=tcod[m][:].bitcast(FP8X4),
+                rhs_scale=tscl[m][:],
+                start=True,
+                stop=True,
+            )
+            return u
+
+        def phase1(m):
+            acc[m] = small.tile([P, 4], F32, name="acc", tag="acc")
+            for a in range(4):
+                u = mx_pass(m, a)
+                j = junkp.tile([P, D], F32, name="junk", tag="junk")
+                nc.scalar.activation(out=j[:], in_=u[:], func=ACT.Square, accum_out=acc[m][:, a : a + 1])
+
+        def total(m):
+            for a in range(4):
+                nc.tensor.matmul(
+                    out=tot[:, m : m + 1], lhsT=ones[:], rhs=acc[m][:, a : a + 1],
+                    start=(a == 0), stop=(a == 3),
+                )
+
+        def chain_relu(m):
+            yrel[m] = small.tile([P, 1], F32, name="yrel", tag="yrel")
+            nc.scalar.activation(
+                out=yrel[m][:], in_=tot[:, m : m + 1], func=ACT.Relu,
+                scale=1.0 / (BUDGET * BUDGET), bias=neg_col[:],
+            )
+
+        def chain_sqrt(m):
+            fsq[m] = small.tile([P, 1], F32, name="fsq", tag="fsq")
+            nc.scalar.activation(out=fsq[m][:], in_=yrel[m][:], func=ACT.Sqrt, bias=one_col[:])
+            sfac[m] = small.tile([P, 1], F32, name="sfac", tag="sfac")
+            nc.vector.reciprocal(out=sfac[m][:], in_=fsq[m][:])
+
+        def phase2(m, a):
+            if a == 0:
+                o_sb[m] = opool.tile([P, 4, D], F32, name="o_sb", tag="o_sb")
+            u = mx_pass(m, a)
+            nc.scalar.activation(out=o_sb[m][:, a, :], in_=u[:], func=ACT.Copy, scale=sfac[m][:, 0:1])
+
+        def store(m):
+            b, k = divmod(m, NB)
+            nc.sync.dma_start(
+                out=out[b, k].rearrange("(m a) n -> m a n", a=4),
+                in_=o_sb[m][:],
+            )
+
+        prep_step(0)
+        prep_step(1)
+        for i in range(NM + 1):
+            prep_step(i + 2)
+            if i < NM:
+                phase1(i)
+            if i >= 1:
+                phase2(i - 1, 0)
+            if i < NM:
+                total(i)
+                chain_relu(i)
+            if i >= 1:
+                phase2(i - 1, 1)
+            if i < NM:
+                chain_sqrt(i)
+            if i >= 1:
+                phase2(i - 1, 2)
+                phase2(i - 1, 3)
+                store(i - 1)

@@ -1,8 +1,6 @@
 from contextlib import ExitStack
 
-import concourse.bass as bass
 import concourse.mybir as mybir
-import concourse.tile as tile
 from concourse.masks import make_identity
 
 F32 = mybir.dt.float32
@@ -18,19 +16,30 @@ D = 512
 NB = 8
 NM = 16
 FREE = 4 * D
+CF = 512
+Q = 32
 BUDGET = 16.0
 
 FLOPS = 2 * NM * D * D * D
 
-W_BUFS = 8
-W_AHEAD = 6
+MANUAL = False
+AHEAD = 2
+
+
+def v_banks(m):
+    if m == NM - 1:
+        return [2, 3]
+    if m >= NM - 3:
+        return [0, 1, 2, 3]
+    return []
 
 
 def tile_proceduralmemory_pb_kernel(tc, W_pm, G, raw_beta, raw_decay, out):
     nc = tc.nc
     with ExitStack() as ctx:
+        if MANUAL:
+            ctx.enter_context(tc.manual_schedule())
         const = ctx.enter_context(tc.tile_pool(name="const", bufs=1))
-        wpool = ctx.enter_context(tc.tile_pool(name="wpool", bufs=W_BUFS))
         stage = ctx.enter_context(tc.tile_pool(name="stage", bufs=3))
         codes = ctx.enter_context(tc.tile_pool(name="codes", bufs=4))
         small = ctx.enter_context(tc.tile_pool(name="small", bufs=4))
@@ -47,9 +56,14 @@ def tile_proceduralmemory_pb_kernel(tc, W_pm, G, raw_beta, raw_decay, out):
 
         g_n = []
         g_r = []
+        g_c = []
         for b in range(2):
             g_n.append(const.tile([P, FREE], BF16, name="g_n%d" % b))
             g_r.append(const.tile([P, FREE], BF16, name="g_r%d" % b))
+            g_c.append(const.tile([P, CF], BF16, name="g_c%d" % b))
+        w_sb = []
+        for m in range(NM):
+            w_sb.append(const.tile([P, FREE], BF16, name="w_sb%d" % m))
 
         def load_g(b):
             nc.sync.dma_start(
@@ -57,40 +71,39 @@ def tile_proceduralmemory_pb_kernel(tc, W_pm, G, raw_beta, raw_decay, out):
                 in_=G[b].rearrange("(u q e) n -> q u (e n)", u=2, e=2),
             )
 
-        w_sb = {}
-
         def load_w(m):
             b, k = divmod(m, NB)
-            t = wpool.tile([P, FREE], BF16, name="w_sb", tag="w_sb")
-            nc.sync.dma_start(out=t[:], in_=W_pm[b, k].rearrange("(p a) j -> p (a j)", a=4))
-            w_sb[m] = t
+            nc.sync.dma_start(out=w_sb[m][:], in_=W_pm[b, k].rearrange("(p a) j -> p (a j)", a=4))
 
         load_g(0)
-        load_w(0)
-        load_w(1)
-        load_w(2)
+        for m in range(4):
+            load_w(m)
         load_g(1)
-        for m in range(3, W_AHEAD):
+        for m in range(4, NM):
             load_w(m)
 
         ident = const.tile([P, P], F32, name="ident")
         make_identity(nc, ident[:])
-        ones = const.tile([P, P], F32, name="ones")
-        nc.vector.memset(ones[:], 1.0)
         one_col = const.tile([P, 1], F32, name="one_col")
         nc.vector.memset(one_col[:], 1.0)
         neg_col = const.tile([P, 1], F32, name="neg_col")
         nc.vector.memset(neg_col[:], -1.0)
-
-        eye_r = const.tile([P, FREE], BF16, name="eye_r")
-        nc.vector.memset(eye_r[:], 0.0)
-        eye_v = eye_r[:].rearrange("p (c n x) -> p c n x", c=2, n=P, x=8)
-        for u in range(2):
-            for e in range(2):
-                nc.vector.tensor_copy(out=eye_v[:, u, :, 5 * e + 2 * u], in_=ident[:])
+        ones = const.tile([P, P], F32, name="ones")
+        nc.vector.memset(ones[:], 1.0)
+        eye_c = const.tile([P, CF], BF16, name="eye_c")
+        nc.vector.memset(eye_c[:], 0.0)
 
         warm = const.tile([P, 1], F32, name="warm")
         nc.scalar.activation(out=warm[:], in_=one_col[:], func=ACT.Exp)
+
+        eye_q = const.tile([P, Q], BF16, name="eye_q")
+        for a in range(4):
+            nc.vector.tensor_copy(out=eye_q[a * Q : (a + 1) * Q, :], in_=ident[a * Q : (a + 1) * Q, a * Q : (a + 1) * Q])
+        eye_v = eye_c[:].rearrange("p (u j x) -> p u j x", u=2, j=Q, x=8)
+        for u in range(2):
+            for e in range(2):
+                nc.vector.tensor_copy(out=eye_v[:, u, :, 5 * e + 2 * u], in_=eye_q[:])
+
         ab = const.tile([P, NB], F32, name="ab")
         nc.scalar.activation(out=ab[:], in_=rb[:], func=ACT.Abs)
         e2 = const.tile([P, NB], F32, name="e2")
@@ -99,33 +112,42 @@ def tile_proceduralmemory_pb_kernel(tc, W_pm, G, raw_beta, raw_decay, out):
         nc.scalar.activation(out=e1[:], in_=ab[:], func=ACT.Exp, scale=-1.0)
         l1 = const.tile([P, NB], F32, name="l1")
         nc.scalar.activation(out=l1[:], in_=e1[:], func=ACT.Ln, bias=one_col[:])
-        warm2 = const.tile([P, 1], F32, name="warm2")
-        nc.scalar.activation(out=warm2[:], in_=l1[:, 0:1], func=ACT.Sqrt, bias=one_col[:])
 
         d1 = const.tile([P, NB], F32, name="d1")
         nc.vector.tensor_scalar_add(out=d1[:], in0=e2[:], scalar1=1.0)
         decay = const.tile([P, NB], F32, name="decay")
         nc.vector.reciprocal(out=decay[:], in_=d1[:])
         beta = const.tile([P, NB], F32, name="beta")
-        nc.vector.scalar_tensor_tensor(
-            out=beta[:], in0=rb[:], scalar=0.0, in1=l1[:], op0=ALU.max, op1=ALU.add
-        )
 
-        dk = []
+        dc = []
         for k in range(NB):
-            dk.append(const.tile([P, FREE], F32, name="dk%d" % k))
+            dc.append(const.tile([P, CF], F32, name="dc%d" % k))
 
         tot = ptot.tile([P, NM], F32, name="tot")
+
+        def band(ap, a):
+            return ap[a * Q : (a + 1) * Q, :].rearrange("p (u a x) -> p u a x", u=2, a=4)[:, :, a, :]
+
+        def compact(ap, a):
+            return ap[a * Q : (a + 1) * Q, :].rearrange("p (u x) -> p u x", u=2)
 
         def regroup_g(b):
             nc.vector.tensor_copy(
                 out=g_r[b][:].rearrange("p (n t) -> p n t", t=4),
                 in_=g_n[b][:].rearrange("p (t n) -> p n t", t=4),
             )
+            for a in range(4):
+                nc.vector.tensor_copy(out=compact(g_c[b], a), in_=band(g_r[b], a))
+
+        def make_dc(k):
+            nc.vector.tensor_scalar(
+                out=dc[k][:], in0=eye_c[:], scalar1=decay[:, k : k + 1], scalar2=None, op0=ALU.mult
+            )
 
         tps = {}
         wg = {}
         tbf = {}
+        tcm = {}
         wcod = {}
         wscl = {}
         tcod = {}
@@ -135,8 +157,11 @@ def tile_proceduralmemory_pb_kernel(tc, W_pm, G, raw_beta, raw_decay, out):
         yrel = {}
         fsq = {}
         o_sb = {}
+        ups = {}
 
         def transposes(m):
+            if m >= NM:
+                return
             x32 = w_sb[m][:].bitcast(F32)
             tiles = []
             for h in range(2):
@@ -149,17 +174,22 @@ def tile_proceduralmemory_pb_kernel(tc, W_pm, G, raw_beta, raw_decay, out):
                 tiles.append(tp)
             tps[m] = tiles
 
-        def evac(m):
+        def evac(m, on_scalar):
+            if m >= NM:
+                return
             g = stage.tile([P, FREE], BF16, name="wg", tag="wg", align_bytes=64)
             g32 = g[:].bitcast(F32).rearrange("p (a m u) -> p a m u", a=4, m=P, u=2)
             for h in range(2):
-                nc.vector.tensor_copy(
-                    out=g32[:, 2 * h : 2 * h + 2],
-                    in_=tps[m][h][:].rearrange("p a u m -> p a m u"),
-                )
+                src = tps[m][h][:].rearrange("p a u m -> p a m u")
+                if on_scalar:
+                    nc.scalar.copy(out=g32[:, 2 * h : 2 * h + 2], in_=src)
+                else:
+                    nc.vector.tensor_copy(out=g32[:, 2 * h : 2 * h + 2], in_=src)
             wg[m] = g
 
         def quant_w(m):
+            if m >= NM:
+                return
             c = codes.tile([P, D], U32, name="wcod", tag="wcod", align_bytes=64)
             s = codes.tile([P, D], U8, name="wscl", tag="wscl", align_bytes=64)
             nc.vector.quantize_mx(out=c[:].bitcast(FP8X4), scales=s[:], in_=wg[m][:])
@@ -167,40 +197,35 @@ def tile_proceduralmemory_pb_kernel(tc, W_pm, G, raw_beta, raw_decay, out):
             wscl[m] = s
 
         def tcomp(m):
+            if m >= NM:
+                return
             b, k = divmod(m, NB)
-            if b == 0:
-                nc.vector.tensor_scalar(
-                    out=dk[k][:], in0=eye_r[:], scalar1=decay[:, k : k + 1], scalar2=None, op0=ALU.mult
-                )
-            t = stage.tile([P, FREE], BF16, name="tbf", tag="tbf", align_bytes=64)
+            tcm[m] = stage.tile([P, CF], BF16, name="tcm", tag="tcm")
             nc.vector.scalar_tensor_tensor(
-                out=t[:], in0=g_r[b][:], scalar=beta[:, k : k + 1], in1=dk[k][:],
+                out=tcm[m][:], in0=g_c[b][:], scalar=beta[:, k : k + 1], in1=dc[k][:],
                 op0=ALU.mult, op1=ALU.add,
             )
-            tbf[m] = t
+            tbf[m] = stage.tile([P, FREE], BF16, name="tbf", tag="tbf", align_bytes=64)
+            nc.vector.tensor_scalar(
+                out=tbf[m][:], in0=g_r[b][:], scalar1=beta[:, k : k + 1], scalar2=None, op0=ALU.mult
+            )
+
+        def tcopies(m):
+            if m >= NM:
+                return
+            for a in range(4):
+                nc.vector.tensor_copy(out=band(tbf[m], a), in_=compact(tcm[m], a))
 
         def quant_t(m):
+            if m >= NM:
+                return
             c = codes.tile([P, D], U32, name="tcod", tag="tcod", align_bytes=64)
             s = codes.tile([P, D], U8, name="tscl", tag="tscl", align_bytes=64)
             nc.vector.quantize_mx(out=c[:].bitcast(FP8X4), scales=s[:], in_=tbf[m][:])
             tcod[m] = c
             tscl[m] = s
 
-        def prep_step(j):
-            if j < NM:
-                if j % NB == 0:
-                    regroup_g(j // NB)
-                transposes(j)
-                if j + W_AHEAD < NM:
-                    load_w(j + W_AHEAD)
-                evac(j)
-            if 1 <= j <= NM:
-                quant_t(j - 1)
-            if j < NM:
-                tcomp(j)
-                quant_w(j)
-
-        def mx_pass(m, a):
+        def mx_pass(m, a, ph):
             u = pu.tile([P, D], F32, name="u", tag="u")
             nc.tensor.matmul_mx(
                 out=u[:],
@@ -211,14 +236,15 @@ def tile_proceduralmemory_pb_kernel(tc, W_pm, G, raw_beta, raw_decay, out):
                 start=True,
                 stop=True,
             )
-            return u
+            ups[(m, a, ph)] = u
 
-        def phase1(m):
-            acc[m] = small.tile([P, 4], F32, name="acc", tag="acc")
-            for a in range(4):
-                u = mx_pass(m, a)
-                j = junkp.tile([P, D], F32, name="junk", tag="junk")
-                nc.scalar.activation(out=j[:], in_=u[:], func=ACT.Square, accum_out=acc[m][:, a : a + 1])
+        def square(m, a):
+            if a == 0:
+                acc[m] = small.tile([P, 4], F32, name="acc", tag="acc")
+            j = junkp.tile([P, D], F32, name="junk", tag="junk")
+            nc.scalar.activation(
+                out=j[:], in_=ups[(m, a, 1)][:], func=ACT.Square, accum_out=acc[m][:, a : a + 1]
+            )
 
         def total(m):
             for a in range(4):
@@ -237,38 +263,94 @@ def tile_proceduralmemory_pb_kernel(tc, W_pm, G, raw_beta, raw_decay, out):
         def chain_sqrt(m):
             fsq[m] = small.tile([P, 1], F32, name="fsq", tag="fsq")
             nc.scalar.activation(out=fsq[m][:], in_=yrel[m][:], func=ACT.Sqrt, bias=one_col[:])
+
+        def chain_recip(m):
             sfac[m] = small.tile([P, 1], F32, name="sfac", tag="sfac")
             nc.vector.reciprocal(out=sfac[m][:], in_=fsq[m][:])
 
-        def phase2(m, a):
-            if a == 0:
+        def scale(m, a, on_vector):
+            if m not in o_sb:
                 o_sb[m] = opool.tile([P, 4, D], F32, name="o_sb", tag="o_sb")
-            u = mx_pass(m, a)
-            nc.scalar.activation(out=o_sb[m][:, a, :], in_=u[:], func=ACT.Copy, scale=sfac[m][:, 0:1])
+            u = ups[(m, a, 2)]
+            if on_vector:
+                nc.vector.tensor_scalar(
+                    out=o_sb[m][:, a, :], in0=u[:], scalar1=sfac[m][:, 0:1], scalar2=None, op0=ALU.mult
+                )
+            else:
+                nc.scalar.activation(out=o_sb[m][:, a, :], in_=u[:], func=ACT.Copy, scale=sfac[m][:, 0:1])
 
-        def store(m):
+        def store(m, a0, a1):
             b, k = divmod(m, NB)
             nc.sync.dma_start(
-                out=out[b, k].rearrange("(m a) n -> m a n", a=4),
-                in_=o_sb[m][:],
+                out=out[b, k].rearrange("(m a) n -> m a n", a=4)[:, a0:a1, :],
+                in_=o_sb[m][:, a0:a1, :],
             )
 
-        prep_step(0)
-        prep_step(1)
+        transposes(0)
+        make_dc(0)
+        regroup_g(0)
+        nc.vector.scalar_tensor_tensor(
+            out=beta[:], in0=rb[:], scalar=0.0, in1=l1[:], op0=ALU.max, op1=ALU.add
+        )
+        evac(0, True)
+        transposes(1)
+        warm2 = const.tile([P, 1], F32, name="warm2")
+        nc.scalar.activation(out=warm2[:], in_=l1[:, 0:1], func=ACT.Sqrt, bias=one_col[:])
+        tcomp(0)
+        tcopies(0)
+        quant_w(0)
+        quant_t(0)
+        evac(1, True)
+        transposes(2)
+        make_dc(1)
+        tcomp(1)
+        tcopies(1)
+        quant_w(1)
+
         for i in range(NM + 1):
-            prep_step(i + 2)
+            j = i + AHEAD
+            p = i - 1
+            vb = v_banks(p) if p >= 0 else []
+            sb = [a for a in range(4) if a not in vb] if p >= 0 else []
+            evac(j, False)
+            quant_t(j - 1)
             if i < NM:
-                phase1(i)
-            if i >= 1:
-                phase2(i - 1, 0)
-            if i < NM:
-                total(i)
-                chain_relu(i)
-            if i >= 1:
-                phase2(i - 1, 1)
-            if i < NM:
-                chain_sqrt(i)
-            if i >= 1:
-                phase2(i - 1, 2)
-                phase2(i - 1, 3)
-                store(i - 1)
+                for a in range(4):
+                    mx_pass(i, a, 1)
+                    square(i, a)
+            if i == NM:
+                for a in (vb[0], sb[0], vb[1], sb[1]):
+                    mx_pass(p, a, 2)
+                for q in range(2):
+                    scale(p, vb[q], True)
+                    scale(p, sb[q], False)
+                store(p, 0, 2)
+                store(p, 2, 4)
+                continue
+            for a in vb:
+                mx_pass(p, a, 2)
+                scale(p, a, True)
+            for a in sb[:1]:
+                mx_pass(p, a, 2)
+                scale(p, a, False)
+            total(i)
+            chain_relu(i)
+            for a in sb[1:2]:
+                mx_pass(p, a, 2)
+                scale(p, a, False)
+            chain_sqrt(i)
+            for a in sb[2:]:
+                mx_pass(p, a, 2)
+                scale(p, a, False)
+            transposes(j + 1)
+            if j < NM:
+                if j == NB:
+                    regroup_g(1)
+                if j < NB:
+                    make_dc(j)
+                tcomp(j)
+                quant_w(j)
+                tcopies(j)
+            if p >= 0:
+                store(p, 0, 4)
+            chain_recip(i)

@@ -31,7 +31,7 @@ def v_banks(m):
         return [2, 3]
     if m >= NM - 3:
         return [0, 1, 2, 3]
-    return []
+    return [0]
 
 
 def tile_proceduralmemory_pb_kernel(tc, W_pm, G, raw_beta, raw_decay, out):

@@ -31,7 +31,7 @@ def v_banks(m):
         return [2, 3]
     if m >= NM - 3:
         return [0, 1, 2, 3]
-    return [0]
+    return []
 
 
 def tile_proceduralmemory_pb_kernel(tc, W_pm, G, raw_beta, raw_decay, out):
@@ -123,7 +123,8 @@ def tile_proceduralmemory_pb_kernel(tc, W_pm, G, raw_beta, raw_decay, out):
         for k in range(NB):
             dc.append(const.tile([P, CF], F32, name="dc%d" % k))
 
-        tot = ptot.tile([P, NM], F32, name="tot")
+        tot = ptot.tile([P, 4 * NM], F32, name="tot")
+        tsum = {}
 
         def band(ap, a):
             return ap[a * Q : (a + 1) * Q, :].rearrange("p (u a x) -> p u a x", u=2, a=4)[:, :, a, :]
@@ -247,16 +248,18 @@ def tile_proceduralmemory_pb_kernel(tc, W_pm, G, raw_beta, raw_decay, out):
             )
 
         def total(m):
-            for a in range(4):
-                nc.tensor.matmul(
-                    out=tot[:, m : m + 1], lhsT=ones[:], rhs=acc[m][:, a : a + 1],
-                    start=(a == 0), stop=(a == 3),
-                )
+            nc.tensor.matmul(
+                out=tot[:, 4 * m : 4 * m + 4], lhsT=ones[:], rhs=acc[m][:, 0:4], start=True, stop=True
+            )
+            tsum[m] = small.tile([P, 1], F32, name="tsum", tag="tsum")
+            nc.vector.tensor_reduce(
+                out=tsum[m][:], in_=tot[:, 4 * m : 4 * m + 4], axis=mybir.AxisListType.X, op=ALU.add
+            )
 
         def chain_relu(m):
             yrel[m] = small.tile([P, 1], F32, name="yrel", tag="yrel")
             nc.scalar.activation(
-                out=yrel[m][:], in_=tot[:, m : m + 1], func=ACT.Relu,
+                out=yrel[m][:], in_=tsum[m][:], func=ACT.Relu,
                 scale=1.0 / (BUDGET * BUDGET), bias=neg_col[:],
             )
 

@@ -22,7 +22,7 @@ BUDGET = 16.0
 
 FLOPS = 2 * NM * D * D * D
 
-MANUAL = False
+MANUAL = True
 AHEAD = 2
 
 
@@ -31,6 +31,10 @@ def v_banks(m):
         return [2, 3]
     if m >= NM - 3:
         return [0, 1, 2, 3]
+    if m >= NM - 4:
+        return [0, 1]
+    if m >= NM - 7:
+        return [0]
     return []
 
 
@@ -123,8 +127,7 @@ def tile_proceduralmemory_pb_kernel(tc, W_pm, G, raw_beta, raw_decay, out):
         for k in range(NB):
             dc.append(const.tile([P, CF], F32, name="dc%d" % k))
 
-        tot = ptot.tile([P, 4 * NM], F32, name="tot")
-        tsum = {}
+        tot = ptot.tile([P, NM], F32, name="tot")
 
         def band(ap, a):
             return ap[a * Q : (a + 1) * Q, :].rearrange("p (u a x) -> p u a x", u=2, a=4)[:, :, a, :]
@@ -247,29 +250,24 @@ def tile_proceduralmemory_pb_kernel(tc, W_pm, G, raw_beta, raw_decay, out):
                 out=j[:], in_=ups[(m, a, 1)][:], func=ACT.Square, accum_out=acc[m][:, a : a + 1]
             )
 
-        def total(m):
+        def total(m, a):
             nc.tensor.matmul(
-                out=tot[:, 4 * m : 4 * m + 4], lhsT=ones[:], rhs=acc[m][:, 0:4], start=True, stop=True
-            )
-            tsum[m] = small.tile([P, 1], F32, name="tsum", tag="tsum")
-            nc.vector.tensor_reduce(
-                out=tsum[m][:], in_=tot[:, 4 * m : 4 * m + 4], axis=mybir.AxisListType.X, op=ALU.add
+                out=tot[:, m : m + 1], lhsT=ones[:], rhs=acc[m][:, a : a + 1],
+                start=(a == 0), stop=(a == 3),
             )
 
         def chain_relu(m):
             yrel[m] = small.tile([P, 1], F32, name="yrel", tag="yrel")
             nc.scalar.activation(
-                out=yrel[m][:], in_=tsum[m][:], func=ACT.Relu,
+                out=yrel[m][:], in_=tot[:, m : m + 1], func=ACT.Relu,
                 scale=1.0 / (BUDGET * BUDGET), bias=neg_col[:],
             )
 
-        def chain_sqrt(m):
-            fsq[m] = small.tile([P, 1], F32, name="fsq", tag="fsq")
-            nc.scalar.activation(out=fsq[m][:], in_=yrel[m][:], func=ACT.Sqrt, bias=one_col[:])
-
-        def chain_recip(m):
+        def chain_rsqrt(m):
             sfac[m] = small.tile([P, 1], F32, name="sfac", tag="sfac")
-            nc.vector.reciprocal(out=sfac[m][:], in_=fsq[m][:])
+            nc.scalar.activation(
+                out=sfac[m][:], in_=yrel[m][:], func=ACT.Abs_reciprocal_sqrt, bias=one_col[:]
+            )
 
         def scale(m, a, on_vector):
             if m not in o_sb:
@@ -290,70 +288,83 @@ def tile_proceduralmemory_pb_kernel(tc, W_pm, G, raw_beta, raw_decay, out):
             )
 
         transposes(0)
-        make_dc(0)
         regroup_g(0)
+        make_dc(0)
         nc.vector.scalar_tensor_tensor(
             out=beta[:], in0=rb[:], scalar=0.0, in1=l1[:], op0=ALU.max, op1=ALU.add
         )
         evac(0, True)
         transposes(1)
         warm2 = const.tile([P, 1], F32, name="warm2")
-        nc.scalar.activation(out=warm2[:], in_=l1[:, 0:1], func=ACT.Sqrt, bias=one_col[:])
+        nc.scalar.activation(out=warm2[:], in_=l1[:, 0:1], func=ACT.Abs_reciprocal_sqrt, bias=one_col[:])
         tcomp(0)
+        make_dc(1)
         tcopies(0)
         quant_w(0)
         quant_t(0)
         evac(1, True)
-        transposes(2)
-        make_dc(1)
         tcomp(1)
-        tcopies(1)
         quant_w(1)
+        tcopies(1)
 
+        pending = []
         for i in range(NM + 1):
             j = i + AHEAD
             p = i - 1
             vb = v_banks(p) if p >= 0 else []
             sb = [a for a in range(4) if a not in vb] if p >= 0 else []
-            evac(j, False)
             quant_t(j - 1)
             if i < NM:
                 for a in range(4):
                     mx_pass(i, a, 1)
                     square(i, a)
+                    if pending and a == 1:
+                        chain_relu(pending[0])
+                    if pending and a == 2:
+                        chain_rsqrt(pending[0])
+                        pending = []
+            if i == 0:
+                transposes(2)
+                evac(2, True)
+            else:
+                transposes(j + 1)
+            order = vb + sb
             if i == NM:
-                for a in (vb[0], sb[0], vb[1], sb[1]):
-                    mx_pass(p, a, 2)
-                for q in range(2):
-                    scale(p, vb[q], True)
-                    scale(p, sb[q], False)
-                store(p, 0, 2)
-                store(p, 2, 4)
-                continue
-            for a in vb:
-                mx_pass(p, a, 2)
-                scale(p, a, True)
-            for a in sb[:1]:
-                mx_pass(p, a, 2)
-                scale(p, a, False)
-            total(i)
-            chain_relu(i)
-            for a in sb[1:2]:
-                mx_pass(p, a, 2)
-                scale(p, a, False)
-            chain_sqrt(i)
-            for a in sb[2:]:
-                mx_pass(p, a, 2)
-                scale(p, a, False)
-            transposes(j + 1)
+                order = [vb[0], sb[0], vb[1], sb[1]]
+            for q in range(4):
+                if p >= 0:
+                    mx_pass(p, order[q], 2)
+                if i < NM:
+                    total(i, q)
+            if i == 0:
+                transposes(j + 1)
+            if i < NM and not sb and i + 1 < NM and p >= 0:
+                pending = [i]
+            else:
+                n_relu = min(3, len(sb))
+                for n in range(len(sb) + 1):
+                    if i < NM and n == n_relu:
+                        chain_relu(i)
+                    if i < NM and n == n_relu + 1:
+                        chain_rsqrt(i)
+                    if n < len(sb):
+                        scale(p, sb[n], False)
+                if i < NM and n_relu == len(sb):
+                    chain_rsqrt(i)
             if j < NM:
                 if j == NB:
                     regroup_g(1)
-                if j < NB:
+                if 2 <= j < NB:
                     make_dc(j)
                 tcomp(j)
-                quant_w(j)
-                tcopies(j)
+            for a in vb:
+                scale(p, a, True)
             if p >= 0:
-                store(p, 0, 4)
-            chain_recip(i)
+                if i == NM:
+                    store(p, 0, 2)
+                    store(p, 2, 4)
+                else:
+                    store(p, 0, 4)
+            quant_w(j)
+            tcopies(j)
+            evac(j + 1, False)

@@ -22,7 +22,7 @@ BUDGET = 16.0
 
 FLOPS = 2 * NM * D * D * D
 
-MANUAL = True
+MANUAL = False
 AHEAD = 2
 
 
@@ -31,10 +31,6 @@ def v_banks(m):
         return [2, 3]
     if m >= NM - 3:
         return [0, 1, 2, 3]
-    if m >= NM - 4:
-        return [0, 1]
-    if m >= NM - 7:
-        return [0]
     return []
 
 
@@ -185,7 +181,7 @@ def tile_proceduralmemory_pb_kernel(tc, W_pm, G, raw_beta, raw_decay, out):
             g32 = g[:].bitcast(F32).rearrange("p (a m u) -> p a m u", a=4, m=P, u=2)
             for h in range(2):
                 src = tps[m][h][:].rearrange("p a u m -> p a m u")
-                if on_scalar:
+                if on_scalar or h == 0:
                     nc.scalar.copy(out=g32[:, 2 * h : 2 * h + 2], in_=src)
                 else:
                     nc.vector.tensor_copy(out=g32[:, 2 * h : 2 * h + 2], in_=src)
@@ -250,11 +246,12 @@ def tile_proceduralmemory_pb_kernel(tc, W_pm, G, raw_beta, raw_decay, out):
                 out=j[:], in_=ups[(m, a, 1)][:], func=ACT.Square, accum_out=acc[m][:, a : a + 1]
             )
 
-        def total(m, a):
-            nc.tensor.matmul(
-                out=tot[:, m : m + 1], lhsT=ones[:], rhs=acc[m][:, a : a + 1],
-                start=(a == 0), stop=(a == 3),
-            )
+        def total(m):
+            for a in range(4):
+                nc.tensor.matmul(
+                    out=tot[:, m : m + 1], lhsT=ones[:], rhs=acc[m][:, a : a + 1],
+                    start=(a == 0), stop=(a == 3),
+                )
 
         def chain_relu(m):
             yrel[m] = small.tile([P, 1], F32, name="yrel", tag="yrel")
@@ -263,7 +260,7 @@ def tile_proceduralmemory_pb_kernel(tc, W_pm, G, raw_beta, raw_decay, out):
                 scale=1.0 / (BUDGET * BUDGET), bias=neg_col[:],
             )
 
-        def chain_rsqrt(m):
+        def chain_sqrt(m):
             sfac[m] = small.tile([P, 1], F32, name="sfac", tag="sfac")
             nc.scalar.activation(
                 out=sfac[m][:], in_=yrel[m][:], func=ACT.Abs_reciprocal_sqrt, bias=one_col[:]
@@ -288,8 +285,8 @@ def tile_proceduralmemory_pb_kernel(tc, W_pm, G, raw_beta, raw_decay, out):
             )
 
         transposes(0)
-        regroup_g(0)
         make_dc(0)
+        regroup_g(0)
         nc.vector.scalar_tensor_tensor(
             out=beta[:], in0=rb[:], scalar=0.0, in1=l1[:], op0=ALU.max, op1=ALU.add
         )
@@ -298,73 +295,59 @@ def tile_proceduralmemory_pb_kernel(tc, W_pm, G, raw_beta, raw_decay, out):
         warm2 = const.tile([P, 1], F32, name="warm2")
         nc.scalar.activation(out=warm2[:], in_=l1[:, 0:1], func=ACT.Abs_reciprocal_sqrt, bias=one_col[:])
         tcomp(0)
-        make_dc(1)
         tcopies(0)
         quant_w(0)
         quant_t(0)
         evac(1, True)
+        transposes(2)
+        make_dc(1)
         tcomp(1)
-        quant_w(1)
         tcopies(1)
+        quant_w(1)
 
-        pending = []
         for i in range(NM + 1):
             j = i + AHEAD
             p = i - 1
             vb = v_banks(p) if p >= 0 else []
             sb = [a for a in range(4) if a not in vb] if p >= 0 else []
+            evac(j, False)
             quant_t(j - 1)
             if i < NM:
                 for a in range(4):
                     mx_pass(i, a, 1)
                     square(i, a)
-                    if pending and a == 1:
-                        chain_relu(pending[0])
-                    if pending and a == 2:
-                        chain_rsqrt(pending[0])
-                        pending = []
-            if i == 0:
-                transposes(2)
-                evac(2, True)
-            else:
-                transposes(j + 1)
-            order = vb + sb
             if i == NM:
-                order = [vb[0], sb[0], vb[1], sb[1]]
-            for q in range(4):
-                if p >= 0:
-                    mx_pass(p, order[q], 2)
-                if i < NM:
-                    total(i, q)
-            if i == 0:
-                transposes(j + 1)
-            if i < NM and not sb and i + 1 < NM and p >= 0:
-                pending = [i]
-            else:
-                n_relu = min(3, len(sb))
-                for n in range(len(sb) + 1):
-                    if i < NM and n == n_relu:
-                        chain_relu(i)
-                    if i < NM and n == n_relu + 1:
-                        chain_rsqrt(i)
-                    if n < len(sb):
-                        scale(p, sb[n], False)
-                if i < NM and n_relu == len(sb):
-                    chain_rsqrt(i)
+                for a in (vb[0], sb[0], vb[1], sb[1]):
+                    mx_pass(p, a, 2)
+                for q in range(2):
+                    scale(p, vb[q], True)
+                    scale(p, sb[q], False)
+                store(p, 0, 2)
+                store(p, 2, 4)
+                continue
+            for a in vb:
+                mx_pass(p, a, 2)
+                scale(p, a, True)
+            for a in sb[:1]:
+                mx_pass(p, a, 2)
+                scale(p, a, False)
+            total(i)
+            chain_relu(i)
+            for a in sb[1:2]:
+                mx_pass(p, a, 2)
+                scale(p, a, False)
+            chain_sqrt(i)
+            for a in sb[2:]:
+                mx_pass(p, a, 2)
+                scale(p, a, False)
+            transposes(j + 1)
             if j < NM:
                 if j == NB:
                     regroup_g(1)
-                if 2 <= j < NB:
+                if j < NB:
                     make_dc(j)
                 tcomp(j)
-            for a in vb:
-                scale(p, a, True)
+                quant_w(j)
+                tcopies(j)
             if p >= 0:
-                if i == NM:
-                    store(p, 0, 2)
-                    store(p, 2, 4)
-                else:
-                    store(p, 0, 4)
-            quant_w(j)
-            tcopies(j)
-            evac(j + 1, False)
+                store(p, 0, 4)

@@ -31,6 +31,8 @@ def v_banks(m):
         return [2, 3]
     if m >= NM - 3:
         return [0, 1, 2, 3]
+    if m >= NM - 10:
+        return [0]
     return []
 
 
@@ -145,13 +147,11 @@ def tile_proceduralmemory_pb_kernel(tc, W_pm, G, raw_beta, raw_decay, out):
             )
 
         tps = {}
-        wg = {}
+        qin = {}
         tbf = {}
         tcm = {}
-        wcod = {}
-        wscl = {}
-        tcod = {}
-        tscl = {}
+        cod = {}
+        scl = {}
         acc = {}
         sfac = {}
         yrel = {}
@@ -177,24 +177,15 @@ def tile_proceduralmemory_pb_kernel(tc, W_pm, G, raw_beta, raw_decay, out):
         def evac(m, on_scalar):
             if m >= NM:
                 return
-            g = stage.tile([P, FREE], BF16, name="wg", tag="wg", align_bytes=64)
-            g32 = g[:].bitcast(F32).rearrange("p (a m u) -> p a m u", a=4, m=P, u=2)
+            g = stage.tile([P, 2 * FREE], BF16, name="qin", tag="qin", align_bytes=64)
+            g32 = g[:, 0:FREE].bitcast(F32).rearrange("p (a m u) -> p a m u", a=4, m=P, u=2)
             for h in range(2):
                 src = tps[m][h][:].rearrange("p a u m -> p a m u")
-                if on_scalar or h == 0:
+                if on_scalar:
                     nc.scalar.copy(out=g32[:, 2 * h : 2 * h + 2], in_=src)
                 else:
                     nc.vector.tensor_copy(out=g32[:, 2 * h : 2 * h + 2], in_=src)
-            wg[m] = g
-
-        def quant_w(m):
-            if m >= NM:
-                return
-            c = codes.tile([P, D], U32, name="wcod", tag="wcod", align_bytes=64)
-            s = codes.tile([P, D], U8, name="wscl", tag="wscl", align_bytes=64)
-            nc.vector.quantize_mx(out=c[:].bitcast(FP8X4), scales=s[:], in_=wg[m][:])
-            wcod[m] = c
-            wscl[m] = s
+            qin[m] = g
 
         def tcomp(m):
             if m >= NM:
@@ -205,9 +196,9 @@ def tile_proceduralmemory_pb_kernel(tc, W_pm, G, raw_beta, raw_decay, out):
                 out=tcm[m][:], in0=g_c[b][:], scalar=beta[:, k : k + 1], in1=dc[k][:],
                 op0=ALU.mult, op1=ALU.add,
             )
-            tbf[m] = stage.tile([P, FREE], BF16, name="tbf", tag="tbf", align_bytes=64)
+            tbf[m] = qin[m][:, FREE : 2 * FREE]
             nc.vector.tensor_scalar(
-                out=tbf[m][:], in0=g_r[b][:], scalar1=beta[:, k : k + 1], scalar2=None, op0=ALU.mult
+                out=tbf[m], in0=g_r[b][:], scalar1=beta[:, k : k + 1], scalar2=None, op0=ALU.mult
             )
 
         def tcopies(m):
@@ -219,20 +210,20 @@ def tile_proceduralmemory_pb_kernel(tc, W_pm, G, raw_beta, raw_decay, out):
         def quant_t(m):
             if m >= NM:
                 return
-            c = codes.tile([P, D], U32, name="tcod", tag="tcod", align_bytes=64)
-            s = codes.tile([P, D], U8, name="tscl", tag="tscl", align_bytes=64)
-            nc.vector.quantize_mx(out=c[:].bitcast(FP8X4), scales=s[:], in_=tbf[m][:])
-            tcod[m] = c
-            tscl[m] = s
+            c = codes.tile([P, 2 * D], U32, name="cod", tag="cod", align_bytes=64)
+            s = codes.tile([P, 2 * D], U8, name="scl", tag="scl", align_bytes=64)
+            nc.vector.quantize_mx(out=c[:].bitcast(FP8X4), scales=s[:], in_=qin[m][:])
+            cod[m] = c
+            scl[m] = s
 
         def mx_pass(m, a, ph):
             u = pu.tile([P, D], F32, name="u", tag="u")
             nc.tensor.matmul_mx(
                 out=u[:],
-                lhsT=wcod[m][:, a * P : (a + 1) * P].bitcast(FP8X4),
-                lhsT_scale=wscl[m][:, a * P : (a + 1) * P],
-                rhs=tcod[m][:].bitcast(FP8X4),
-                rhs_scale=tscl[m][:],
+                lhsT=cod[m][:, a * P : (a + 1) * P].bitcast(FP8X4),
+                lhsT_scale=scl[m][:, a * P : (a + 1) * P],
+                rhs=cod[m][:, D : 2 * D].bitcast(FP8X4),
+                rhs_scale=scl[m][:, D : 2 * D],
                 start=True,
                 stop=True,
             )
@@ -296,14 +287,12 @@ def tile_proceduralmemory_pb_kernel(tc, W_pm, G, raw_beta, raw_decay, out):
         nc.scalar.activation(out=warm2[:], in_=l1[:, 0:1], func=ACT.Abs_reciprocal_sqrt, bias=one_col[:])
         tcomp(0)
         tcopies(0)
-        quant_w(0)
         quant_t(0)
         evac(1, True)
         transposes(2)
         make_dc(1)
         tcomp(1)
         tcopies(1)
-        quant_w(1)
 
         for i in range(NM + 1):
             j = i + AHEAD
@@ -347,7 +336,6 @@ def tile_proceduralmemory_pb_kernel(tc, W_pm, G, raw_beta, raw_decay, out):
                 if j < NB:
                     make_dc(j)
                 tcomp(j)
-                quant_w(j)
                 tcopies(j)
             if p >= 0:
                 store(p, 0, 4)

@@ -31,8 +31,6 @@ def v_banks(m):
         return [2, 3]
     if m >= NM - 3:
         return [0, 1, 2, 3]
-    if m >= NM - 10:
-        return [0]
     return []
 
 
@@ -88,8 +86,8 @@ def tile_proceduralmemory_pb_kernel(tc, W_pm, G, raw_beta, raw_decay, out):
         make_identity(nc, ident[:])
         one_col = const.tile([P, 1], F32, name="one_col")
         nc.vector.memset(one_col[:], 1.0)
-        neg_col = const.tile([P, 1], F32, name="neg_col")
-        nc.vector.memset(neg_col[:], -1.0)
+        neg_half = const.tile([P, 1], F32, name="neg_half")
+        nc.vector.memset(neg_half[:], -0.5)
         ones = const.tile([P, P], F32, name="ones")
         nc.vector.memset(ones[:], 1.0)
         eye_c = const.tile([P, CF], BF16, name="eye_c")
@@ -147,11 +145,13 @@ def tile_proceduralmemory_pb_kernel(tc, W_pm, G, raw_beta, raw_decay, out):
             )
 
         tps = {}
-        qin = {}
+        wg = {}
         tbf = {}
         tcm = {}
-        cod = {}
-        scl = {}
+        wcod = {}
+        wscl = {}
+        tcod = {}
+        tscl = {}
         acc = {}
         sfac = {}
         yrel = {}
@@ -177,15 +177,24 @@ def tile_proceduralmemory_pb_kernel(tc, W_pm, G, raw_beta, raw_decay, out):
         def evac(m, on_scalar):
             if m >= NM:
                 return
-            g = stage.tile([P, 2 * FREE], BF16, name="qin", tag="qin", align_bytes=64)
-            g32 = g[:, 0:FREE].bitcast(F32).rearrange("p (a m u) -> p a m u", a=4, m=P, u=2)
-            for h in range(2):
+            g = stage.tile([P, FREE], BF16, name="wg", tag="wg", align_bytes=64)
+            g32 = g[:].bitcast(F32).rearrange("p (a m u) -> p a m u", a=4, m=P, u=2)
+            for h in (1, 0):
                 src = tps[m][h][:].rearrange("p a u m -> p a m u")
                 if on_scalar:
                     nc.scalar.copy(out=g32[:, 2 * h : 2 * h + 2], in_=src)
                 else:
                     nc.vector.tensor_copy(out=g32[:, 2 * h : 2 * h + 2], in_=src)
-            qin[m] = g
+            wg[m] = g
+
+        def quant_w(m):
+            if m >= NM:
+                return
+            c = codes.tile([P, D], U32, name="wcod", tag="wcod", align_bytes=64)
+            s = codes.tile([P, D], U8, name="wscl", tag="wscl", align_bytes=64)
+            nc.vector.quantize_mx(out=c[:].bitcast(FP8X4), scales=s[:], in_=wg[m][:])
+            wcod[m] = c
+            wscl[m] = s
 
         def tcomp(m):
             if m >= NM:
@@ -196,9 +205,9 @@ def tile_proceduralmemory_pb_kernel(tc, W_pm, G, raw_beta, raw_decay, out):
                 out=tcm[m][:], in0=g_c[b][:], scalar=beta[:, k : k + 1], in1=dc[k][:],
                 op0=ALU.mult, op1=ALU.add,
             )
-            tbf[m] = qin[m][:, FREE : 2 * FREE]
+            tbf[m] = stage.tile([P, FREE], BF16, name="tbf", tag="tbf", align_bytes=64)
             nc.vector.tensor_scalar(
-                out=tbf[m], in0=g_r[b][:], scalar1=beta[:, k : k + 1], scalar2=None, op0=ALU.mult
+                out=tbf[m][:], in0=g_r[b][:], scalar1=beta[:, k : k + 1], scalar2=None, op0=ALU.mult
             )
 
         def tcopies(m):
@@ -210,28 +219,26 @@ def tile_proceduralmemory_pb_kernel(tc, W_pm, G, raw_beta, raw_decay, out):
         def quant_t(m):
             if m >= NM:
                 return
-            c = codes.tile([P, 2 * D], U32, name="cod", tag="cod", align_bytes=64)
-            s = codes.tile([P, 2 * D], U8, name="scl", tag="scl", align_bytes=64)
-            nc.vector.quantize_mx(out=c[:].bitcast(FP8X4), scales=s[:], in_=qin[m][:])
-            cod[m] = c
-            scl[m] = s
+            c = codes.tile([P, D], U32, name="tcod", tag="tcod", align_bytes=64)
+            s = codes.tile([P, D], U8, name="tscl", tag="tscl", align_bytes=64)
+            nc.vector.quantize_mx(out=c[:].bitcast(FP8X4), scales=s[:], in_=tbf[m][:])
+            tcod[m] = c
+            tscl[m] = s
 
         def mx_pass(m, a, ph):
             u = pu.tile([P, D], F32, name="u", tag="u")
             nc.tensor.matmul_mx(
                 out=u[:],
-                lhsT=cod[m][:, a * P : (a + 1) * P].bitcast(FP8X4),
-                lhsT_scale=scl[m][:, a * P : (a + 1) * P],
-                rhs=cod[m][:, D : 2 * D].bitcast(FP8X4),
-                rhs_scale=scl[m][:, D : 2 * D],
+                lhsT=wcod[m][:, a * P : (a + 1) * P].bitcast(FP8X4),
+                lhsT_scale=wscl[m][:, a * P : (a + 1) * P],
+                rhs=tcod[m][:].bitcast(FP8X4),
+                rhs_scale=tscl[m][:],
                 start=True,
                 stop=True,
             )
             ups[(m, a, ph)] = u
 
         def square(m, a):
-            if a == 0:
-                acc[m] = small.tile([P, 4], F32, name="acc", tag="acc")
             j = junkp.tile([P, D], F32, name="junk", tag="junk")
             nc.scalar.activation(
                 out=j[:], in_=ups[(m, a, 1)][:], func=ACT.Square, accum_out=acc[m][:, a : a + 1]
@@ -244,18 +251,14 @@ def tile_proceduralmemory_pb_kernel(tc, W_pm, G, raw_beta, raw_decay, out):
                     start=(a == 0), stop=(a == 3),
                 )
 
-        def chain_relu(m):
+        def chain(m):
             yrel[m] = small.tile([P, 1], F32, name="yrel", tag="yrel")
-            nc.scalar.activation(
-                out=yrel[m][:], in_=tot[:, m : m + 1], func=ACT.Relu,
-                scale=1.0 / (BUDGET * BUDGET), bias=neg_col[:],
+            nc.vector.tensor_scalar(
+                out=yrel[m][:], in0=tot[:, m : m + 1], scalar1=1.0 / (BUDGET * BUDGET), scalar2=1.0,
+                op0=ALU.mult, op1=ALU.max,
             )
-
-        def chain_sqrt(m):
             sfac[m] = small.tile([P, 1], F32, name="sfac", tag="sfac")
-            nc.scalar.activation(
-                out=sfac[m][:], in_=yrel[m][:], func=ACT.Abs_reciprocal_sqrt, bias=one_col[:]
-            )
+            nc.gpsimd.tensor_tensor(out=sfac[m][:], in0=yrel[m][:], in1=neg_half[:], op=ALU.pow)
 
         def scale(m, a, on_vector):
             if m not in o_sb:
@@ -283,16 +286,16 @@ def tile_proceduralmemory_pb_kernel(tc, W_pm, G, raw_beta, raw_decay, out):
         )
         evac(0, True)
         transposes(1)
-        warm2 = const.tile([P, 1], F32, name="warm2")
-        nc.scalar.activation(out=warm2[:], in_=l1[:, 0:1], func=ACT.Abs_reciprocal_sqrt, bias=one_col[:])
         tcomp(0)
         tcopies(0)
+        quant_w(0)
         quant_t(0)
         evac(1, True)
         transposes(2)
         make_dc(1)
         tcomp(1)
         tcopies(1)
+        quant_w(1)
 
         for i in range(NM + 1):
             j = i + AHEAD
@@ -302,33 +305,37 @@ def tile_proceduralmemory_pb_kernel(tc, W_pm, G, raw_beta, raw_decay, out):
             evac(j, False)
             quant_t(j - 1)
             if i < NM:
-                for a in range(4):
+                acc[i] = small.tile([P, 4], F32, name="acc", tag="acc")
+                for a in (0, 2):
                     mx_pass(i, a, 1)
+                    mx_pass(i, a + 1, 1)
+                    square(i, a + 1)
                     square(i, a)
             if i == NM:
-                for a in (vb[0], sb[0], vb[1], sb[1]):
+                for a in (vb[0], vb[1], sb[0], sb[1]):
                     mx_pass(p, a, 2)
-                for q in range(2):
+                for q in (1, 0):
                     scale(p, vb[q], True)
                     scale(p, sb[q], False)
                 store(p, 0, 2)
                 store(p, 2, 4)
                 continue
-            for a in vb:
-                mx_pass(p, a, 2)
-                scale(p, a, True)
-            for a in sb[:1]:
-                mx_pass(p, a, 2)
-                scale(p, a, False)
-            total(i)
-            chain_relu(i)
-            for a in sb[1:2]:
-                mx_pass(p, a, 2)
-                scale(p, a, False)
-            chain_sqrt(i)
-            for a in sb[2:]:
-                mx_pass(p, a, 2)
-                scale(p, a, False)
+            for q in range(0, len(vb), 2):
+                mx_pass(p, vb[q], 2)
+                mx_pass(p, vb[q + 1], 2)
+                scale(p, vb[q + 1], True)
+                scale(p, vb[q], True)
+            for q in range(0, len(sb), 2):
+                mx_pass(p, sb[q], 2)
+                mx_pass(p, sb[q + 1], 2)
+                scale(p, sb[q + 1], False)
+                scale(p, sb[q], False)
+                if q == 0:
+                    total(i)
+                    chain(i)
+            if not sb:
+                total(i)
+                chain(i)
             transposes(j + 1)
             if j < NM:
                 if j == NB:
@@ -336,6 +343,7 @@ def tile_proceduralmemory_pb_kernel(tc, W_pm, G, raw_beta, raw_decay, out):
                 if j < NB:
                     make_dc(j)
                 tcomp(j)
+                quant_w(j)
                 tcopies(j)
             if p >= 0:
                 store(p, 0, 4)

from contextlib import ExitStack

import concourse.mybir as mybir
from concourse.masks import make_identity

F32 = mybir.dt.float32
BF16 = mybir.dt.bfloat16
U32 = mybir.dt.uint32
U8 = mybir.dt.uint8
FP8X4 = mybir.dt.float8_e4m3fn_x4
ACT = mybir.ActivationFunctionType
ALU = mybir.AluOpType

P = 128
D = 512
NB = 8
NM = 16
FREE = 4 * D
CF = 512
Q = 32
BUDGET = 16.0

FLOPS = 2 * NM * D * D * D

MANUAL = False
AHEAD = 2


def v_banks(m):
    if m == NM - 1:
        return [2, 3]
    if m >= NM - 3:
        return [0, 1, 2, 3]
    return []


def tile_proceduralmemory_pb_kernel(tc, W_pm, G, raw_beta, raw_decay, out):
    nc = tc.nc
    with ExitStack() as ctx:
        if MANUAL:
            ctx.enter_context(tc.manual_schedule())
        const = ctx.enter_context(tc.tile_pool(name="const", bufs=1))
        stage = ctx.enter_context(tc.tile_pool(name="stage", bufs=3))
        codes = ctx.enter_context(tc.tile_pool(name="codes", bufs=4))
        small = ctx.enter_context(tc.tile_pool(name="small", bufs=4))
        opool = ctx.enter_context(tc.tile_pool(name="opool", bufs=4))
        junkp = ctx.enter_context(tc.tile_pool(name="junkp", bufs=2))
        ptp = ctx.enter_context(tc.psum_pool(name="ptp", bufs=2))
        pu = ctx.enter_context(tc.psum_pool(name="pu", bufs=5))
        ptot = ctx.enter_context(tc.psum_pool(name="ptot", bufs=1))

        rb = const.tile([P, NB], BF16, name="rb")
        rd = const.tile([P, NB], BF16, name="rd")
        nc.scalar.dma_start(out=rb[:], in_=raw_beta.partition_broadcast(P))
        nc.scalar.dma_start(out=rd[:], in_=raw_decay.partition_broadcast(P))

        g_n = []
        g_r = []
        g_c = []
        for b in range(2):
            g_n.append(const.tile([P, FREE], BF16, name="g_n%d" % b))
            g_r.append(const.tile([P, FREE], BF16, name="g_r%d" % b))
            g_c.append(const.tile([P, CF], BF16, name="g_c%d" % b))
        w_sb = []
        for m in range(NM):
            w_sb.append(const.tile([P, FREE], BF16, name="w_sb%d" % m))

        def load_g(b):
            nc.sync.dma_start(
                out=g_n[b][:].rearrange("p (u x) -> p u x", u=2),
                in_=G[b].rearrange("(u q e) n -> q u (e n)", u=2, e=2),
            )

        def load_w(m):
            b, k = divmod(m, NB)
            nc.sync.dma_start(out=w_sb[m][:], in_=W_pm[b, k].rearrange("(p a) j -> p (a j)", a=4))

        load_g(0)
        for m in range(4):
            load_w(m)
        load_g(1)
        for m in range(4, NM):
            load_w(m)

        ident = const.tile([P, P], F32, name="ident")
        make_identity(nc, ident[:])
        one_col = const.tile([P, 1], F32, name="one_col")
        nc.vector.memset(one_col[:], 1.0)
        neg_half = const.tile([P, 1], F32, name="neg_half")
        nc.vector.memset(neg_half[:], -0.5)
        ones = const.tile([P, P], F32, name="ones")
        nc.vector.memset(ones[:], 1.0)
        eye_c = const.tile([P, CF], BF16, name="eye_c")
        nc.vector.memset(eye_c[:], 0.0)

        warm = const.tile([P, 1], F32, name="warm")
        nc.scalar.activation(out=warm[:], in_=one_col[:], func=ACT.Exp)

        eye_q = const.tile([P, Q], BF16, name="eye_q")
        for a in range(4):
            nc.vector.tensor_copy(out=eye_q[a * Q : (a + 1) * Q, :], in_=ident[a * Q : (a + 1) * Q, a * Q : (a + 1) * Q])
        eye_v = eye_c[:].rearrange("p (u j x) -> p u j x", u=2, j=Q, x=8)
        for u in range(2):
            for e in range(2):
                nc.vector.tensor_copy(out=eye_v[:, u, :, 5 * e + 2 * u], in_=eye_q[:])

        ab = const.tile([P, NB], F32, name="ab")
        nc.scalar.activation(out=ab[:], in_=rb[:], func=ACT.Abs)
        e2 = const.tile([P, NB], F32, name="e2")
        nc.scalar.activation(out=e2[:], in_=rd[:], func=ACT.Exp, scale=-1.0)
        e1 = const.tile([P, NB], F32, name="e1")
        nc.scalar.activation(out=e1[:], in_=ab[:], func=ACT.Exp, scale=-1.0)
        l1 = const.tile([P, NB], F32, name="l1")
        nc.scalar.activation(out=l1[:], in_=e1[:], func=ACT.Ln, bias=one_col[:])

        d1 = const.tile([P, NB], F32, name="d1")
        nc.vector.tensor_scalar_add(out=d1[:], in0=e2[:], scalar1=1.0)
        decay = const.tile([P, NB], F32, name="decay")
        nc.vector.reciprocal(out=decay[:], in_=d1[:])
        beta = const.tile([P, NB], F32, name="beta")

        dc = []
        for k in range(NB):
            dc.append(const.tile([P, CF], F32, name="dc%d" % k))

        tot = ptot.tile([P, NM], F32, name="tot")

        def band(ap, a):
            return ap[a * Q : (a + 1) * Q, :].rearrange("p (u a x) -> p u a x", u=2, a=4)[:, :, a, :]

        def compact(ap, a):
            return ap[a * Q : (a + 1) * Q, :].rearrange("p (u x) -> p u x", u=2)

        def regroup_g(b):
            nc.vector.tensor_copy(
                out=g_r[b][:].rearrange("p (n t) -> p n t", t=4),
                in_=g_n[b][:].rearrange("p (t n) -> p n t", t=4),
            )
            for a in range(4):
                nc.vector.tensor_copy(out=compact(g_c[b], a), in_=band(g_r[b], a))

        def make_dc(k):
            nc.vector.tensor_scalar(
                out=dc[k][:], in0=eye_c[:], scalar1=decay[:, k : k + 1], scalar2=None, op0=ALU.mult
            )

        tps = {}
        wg = {}
        tbf = {}
        tcm = {}
        wcod = {}
        wscl = {}
        tcod = {}
        tscl = {}
        acc = {}
        sfac = {}
        yrel = {}
        fsq = {}
        o_sb = {}
        ups = {}

        def transposes(m):
            if m >= NM:
                return
            x32 = w_sb[m][:].bitcast(F32)
            tiles = []
            for h in range(2):
                tp = ptp.tile([P, 2, 2, P], F32, name="tp", tag="tp")
                for al in range(2):
                    a = 2 * h + al
                    for u in range(2):
                        c0 = a * 256 + u * P
                        nc.tensor.transpose(tp[:, al, u, :], x32[:, c0 : c0 + P], ident[:])
                tiles.append(tp)
            tps[m] = tiles

        def evac(m, on_scalar):
            if m >= NM:
                return
            g = stage.tile([P, FREE], BF16, name="wg", tag="wg", align_bytes=64)
            g32 = g[:].bitcast(F32).rearrange("p (a m u) -> p a m u", a=4, m=P, u=2)
            for h in (1, 0):
                src = tps[m][h][:].rearrange("p a u m -> p a m u")
                if on_scalar:
                    nc.scalar.copy(out=g32[:, 2 * h : 2 * h + 2], in_=src)
                else:
                    nc.vector.tensor_copy(out=g32[:, 2 * h : 2 * h + 2], in_=src)
            wg[m] = g

        def quant_w(m):
            if m >= NM:
                return
            c = codes.tile([P, D], U32, name="wcod", tag="wcod", align_bytes=64)
            s = codes.tile([P, D], U8, name="wscl", tag="wscl", align_bytes=64)
            nc.vector.quantize_mx(out=c[:].bitcast(FP8X4), scales=s[:], in_=wg[m][:])
            wcod[m] = c
            wscl[m] = s

        def tcomp(m):
            if m >= NM:
                return
            b, k = divmod(m, NB)
            tcm[m] = stage.tile([P, CF], BF16, name="tcm", tag="tcm")
            nc.vector.scalar_tensor_tensor(
                out=tcm[m][:], in0=g_c[b][:], scalar=beta[:, k : k + 1], in1=dc[k][:],
                op0=ALU.mult, op1=ALU.add,
            )
            tbf[m] = stage.tile([P, FREE], BF16, name="tbf", tag="tbf", align_bytes=64)
            nc.vector.tensor_scalar(
                out=tbf[m][:], in0=g_r[b][:], scalar1=beta[:, k : k + 1], scalar2=None, op0=ALU.mult
            )

        def tcopies(m):
            if m >= NM:
                return
            for a in range(4):
                nc.vector.tensor_copy(out=band(tbf[m], a), in_=compact(tcm[m], a))

        def quant_t(m):
            if m >= NM:
                return
            c = codes.tile([P, D], U32, name="tcod", tag="tcod", align_bytes=64)
            s = codes.tile([P, D], U8, name="tscl", tag="tscl", align_bytes=64)
            nc.vector.quantize_mx(out=c[:].bitcast(FP8X4), scales=s[:], in_=tbf[m][:])
            tcod[m] = c
            tscl[m] = s

        def mx_pass(m, a, ph):
            u = pu.tile([P, D], F32, name="u", tag="u")
            nc.tensor.matmul_mx(
                out=u[:],
                lhsT=wcod[m][:, a * P : (a + 1) * P].bitcast(FP8X4),
                lhsT_scale=wscl[m][:, a * P : (a + 1) * P],
                rhs=tcod[m][:].bitcast(FP8X4),
                rhs_scale=tscl[m][:],
                start=True,
                stop=True,
            )
            ups[(m, a, ph)] = u

        def square(m, a):
            j = junkp.tile([P, D], F32, name="junk", tag="junk")
            nc.scalar.activation(
                out=j[:], in_=ups[(m, a, 1)][:], func=ACT.Square, accum_out=acc[m][:, a : a + 1]
            )

        def total(m):
            for a in range(4):
                nc.tensor.matmul(
                    out=tot[:, m : m + 1], lhsT=ones[:], rhs=acc[m][:, a : a + 1],
                    start=(a == 0), stop=(a == 3),
                )

        def chain(m):
            yrel[m] = small.tile([P, 1], F32, name="yrel", tag="yrel")
            nc.vector.tensor_scalar(
                out=yrel[m][:], in0=tot[:, m : m + 1], scalar1=1.0 / (BUDGET * BUDGET), scalar2=1.0,
                op0=ALU.mult, op1=ALU.max,
            )
            sfac[m] = small.tile([P, 1], F32, name="sfac", tag="sfac")
            nc.gpsimd.tensor_tensor(out=sfac[m][:], in0=yrel[m][:], in1=neg_half[:], op=ALU.pow)

        def scale(m, a, on_vector):
            if m not in o_sb:
                o_sb[m] = opool.tile([P, 4, D], F32, name="o_sb", tag="o_sb")
            u = ups[(m, a, 2)]
            if on_vector:
                nc.vector.tensor_scalar(
                    out=o_sb[m][:, a, :], in0=u[:], scalar1=sfac[m][:, 0:1], scalar2=None, op0=ALU.mult
                )
            else:
                nc.scalar.activation(out=o_sb[m][:, a, :], in_=u[:], func=ACT.Copy, scale=sfac[m][:, 0:1])

        def store(m, a0, a1):
            b, k = divmod(m, NB)
            nc.sync.dma_start(
                out=out[b, k].rearrange("(m a) n -> m a n", a=4)[:, a0:a1, :],
                in_=o_sb[m][:, a0:a1, :],
            )

        transposes(0)
        make_dc(0)
        regroup_g(0)
        nc.vector.scalar_tensor_tensor(
            out=beta[:], in0=rb[:], scalar=0.0, in1=l1[:], op0=ALU.max, op1=ALU.add
        )
        evac(0, True)
        transposes(1)
        tcomp(0)
        tcopies(0)
        quant_w(0)
        quant_t(0)
        evac(1, True)
        transposes(2)
        make_dc(1)
        tcomp(1)
        tcopies(1)
        quant_w(1)

        for i in range(NM + 1):
            j = i + AHEAD
            p = i - 1
            vb = v_banks(p) if p >= 0 else []
            sb = [a for a in range(4) if a not in vb] if p >= 0 else []
            evac(j, False)
            quant_t(j - 1)
            if i < NM:
                acc[i] = small.tile([P, 4], F32, name="acc", tag="acc")
                for a in (0, 2):
                    mx_pass(i, a, 1)
                    mx_pass(i, a + 1, 1)
                    square(i, a + 1)
                    square(i, a)
            if i == NM:
                for a in (vb[0], vb[1], sb[0], sb[1]):
                    mx_pass(p, a, 2)
                for q in (1, 0):
                    scale(p, vb[q], True)
                    scale(p, sb[q], False)
                store(p, 0, 2)
                store(p, 2, 4)
                continue
            for q in range(0, len(vb), 2):
                mx_pass(p, vb[q], 2)
                mx_pass(p, vb[q + 1], 2)
                scale(p, vb[q + 1], True)
                scale(p, vb[q], True)
            for q in range(0, len(sb), 2):
                mx_pass(p, sb[q], 2)
                mx_pass(p, sb[q + 1], 2)
                scale(p, sb[q + 1], False)
                scale(p, sb[q], False)
                if q == 0:
                    total(i)
                    chain(i)
            if not sb:
                total(i)
                chain(i)
            transposes(j + 1)
            if j < NM:
                if j == NB:
                    regroup_g(1)
                if j < NB:
                    make_dc(j)
                tcomp(j)
                quant_w(j)
                tcopies(j)
            if p >= 0:
                store(p, 0, 4)
